import numpy as np
import ml_dtypes


def mxq(x, axis, fmt="e4m3"):
    dtype, down = {"e4m3": (ml_dtypes.float8_e4m3fn, 7), "e5m2": (ml_dtypes.float8_e5m2, 14)}[fmt]
    v = np.moveaxis(np.asarray(x, np.float32).astype(ml_dtypes.bfloat16).astype(np.float64), axis, -1)
    blocks = v.reshape(v.shape[:-1] + (-1, 32))
    amax = np.abs(blocks).max(-1, keepdims=True)
    byte = np.maximum(np.where(amax > 0, np.frexp(amax)[1] - 1 + 127, 0) - down, 1)
    scale = np.exp2(byte - 127.0)
    codes = (blocks / scale).astype(np.float32).astype(dtype).astype(np.float64)
    return np.moveaxis((codes * scale).reshape(v.shape), -1, axis)


WIDE = False


def mx_kscale(k):
    if not WIDE:
        return np.ones(k)
    levels = np.array([10, -10, 5, -5, 0])
    a = np.random.permutation(np.resize(levels, k // 512 * 4)).reshape(k // 512, 4)
    idx = np.arange(k)
    return np.exp2(a[idx // 512, idx % 128 // 32])


BF16 = ml_dtypes.bfloat16


def bf(x):
    return np.asarray(x, np.float32).astype(BF16)


def f64(x):
    return np.asarray(x).astype(np.float64)


B, S, E, H, DH, ROT, MP = 2, 512, 1024, 8, 128, 32, 4
HD = H * DH
LOC = HD // MP


def rope_sincos():
    inv_freq = 1.0 / (10000.0 ** (np.arange(0, ROT, 2) / ROT))
    ang = np.arange(S)[:, None] * inv_freq[None, :]
    return np.sin(ang), np.cos(ang)


def apply_rope(x, sin, cos):
    sin2 = np.repeat(sin, 2, axis=-1)[None, :, None, :]
    cos2 = np.repeat(cos, 2, axis=-1)[None, :, None, :]
    x1 = x[..., ::2]
    x2 = x[..., 1::2]
    rot = np.stack((-x2, x1), axis=-1).reshape(x.shape)
    return x * cos2 + rot * sin2


def setup_inputs():
    s = mx_kscale(E)
    return {"hidden_states": bf(np.random.standard_normal((B, S, E)) * s),
            "W_qkv": bf(np.random.standard_normal((3 * HD, E)) / np.sqrt(E) / s[None, :])}


def reference(hidden_states, W_qkv):
    qkv = mxq(f64(hidden_states), 2, "e4m3") @ mxq(f64(W_qkv).T, 0, "e4m3")
    qkv = qkv.reshape(B, S, MP, 3 * LOC)
    q, k, v = np.split(qkv, 3, axis=-1)
    q = q.reshape(B, S, H, DH)
    k = k.reshape(B, S, H, DH)
    v = v.reshape(B, S, H, DH)
    sin, cos = rope_sincos()
    q = np.concatenate([apply_rope(q[..., :ROT], sin, cos), q[..., ROT:]], axis=-1)
    k = np.concatenate([apply_rope(k[..., :ROT], sin, cos), k[..., ROT:]], axis=-1)
    return q, k, v

@@ -1,0 +1,247 @@
+import math
+from contextlib import ExitStack
+
+import concourse.mybir as mybir
+from concourse.masks import make_identity
+
+F32 = mybir.dt.float32
+BF16 = mybir.dt.bfloat16
+I32 = mybir.dt.int32
+U32 = mybir.dt.uint32
+U8 = mybir.dt.uint8
+FP8X4 = mybir.dt.float8_e4m3fn_x4
+ALU = mybir.AluOpType
+ACT = mybir.ActivationFunctionType
+
+P = 128
+SEQ = 512
+TOKENS = 2 * SEQ
+TOKEN_TILES = TOKENS // P
+E = 1024
+WORDS = E // 2
+PASSES = E // 512
+HEADS = 8
+DH = 128
+ROT = 32
+PAIRS = ROT // 2
+WIDTH = HEADS * DH
+GROUPS = 4
+GROUP_ROWS = WIDTH // GROUPS
+HALVES = 2
+HALF = WIDTH // HALVES
+Q, K, V = 0, 1, 2
+ORDER = (V, Q, K)
+
+FLOPS = 2 * TOKENS * E * 3 * WIDTH
+
+ROUND_MAGIC = 1.5 * 2.0**23
+TURN_HI = 6.28125
+TURN_LO = 2.0 * math.pi - TURN_HI
+
+
+def build_rope_tables(nc, pool):
+    token = pool.tile([P, TOKEN_TILES], I32, name="token")
+    nc.gpsimd.iota(token[:], pattern=[[1, TOKEN_TILES]], base=0, channel_multiplier=TOKEN_TILES)
+    position_i = pool.tile([P, TOKEN_TILES], I32, name="position_i")
+    nc.vector.tensor_single_scalar(out=position_i[:], in_=token[:], scalar=SEQ - 1, op=ALU.bitwise_and)
+    position = pool.tile([P, TOKEN_TILES], F32, name="position")
+    nc.vector.tensor_copy(out=position[:], in_=position_i[:])
+
+    shape = [P, TOKEN_TILES, PAIRS]
+    angle = pool.tile(shape, F32, name="angle")
+    for j in range(PAIRS):
+        nc.vector.tensor_scalar_mul(
+            out=angle[:, :, j], in0=position[:], scalar1=10000.0 ** (-2.0 * j / ROT)
+        )
+    turns = pool.tile(shape, F32, name="turns")
+    nc.vector.tensor_scalar(
+        out=turns[:], in0=angle[:], scalar1=0.5 / math.pi, scalar2=ROUND_MAGIC,
+        op0=ALU.mult, op1=ALU.add,
+    )
+    nc.vector.tensor_scalar_sub(out=turns[:], in0=turns[:], scalar1=ROUND_MAGIC)
+    partly = pool.tile(shape, F32, name="partly")
+    nc.vector.scalar_tensor_tensor(
+        out=partly[:], in0=turns[:], scalar=-TURN_HI, in1=angle[:], op0=ALU.mult, op1=ALU.add
+    )
+    reduced = pool.tile(shape, F32, name="reduced")
+    nc.vector.scalar_tensor_tensor(
+        out=reduced[:], in0=turns[:], scalar=-TURN_LO, in1=partly[:], op0=ALU.mult, op1=ALU.add
+    )
+    sin_half = pool.tile(shape, F32, name="sin_half")
+    nc.scalar.activation(out=sin_half[:], in_=reduced[:], func=ACT.Sin, scale=0.5)
+    size = pool.tile(shape, F32, name="size")
+    nc.vector.scalar_tensor_tensor(
+        out=size[:], in0=reduced[:], scalar=-1.0, in1=reduced[:], op0=ALU.mult, op1=ALU.max
+    )
+    nc.vector.tensor_scalar(
+        out=size[:], in0=size[:], scalar1=-0.5, scalar2=0.5 * math.pi, op0=ALU.mult, op1=ALU.add
+    )
+    cos_half = pool.tile(shape, F32, name="cos_half")
+    nc.scalar.activation(out=cos_half[:], in_=size[:], func=ACT.Sin)
+
+    table = pool.tile([P, TOKEN_TILES, 2, ROT], F32, name="table")
+    entry = table[:].rearrange("p t r (j c) -> p t r j c", c=2)
+    nc.vector.scalar_tensor_tensor(
+        out=entry[:, :, 1, :, 0], in0=sin_half[:], scalar=2.0, in1=cos_half[:],
+        op0=ALU.mult, op1=ALU.mult,
+    )
+    nc.vector.scalar_tensor_tensor(
+        out=entry[:, :, 0, :, 1], in0=sin_half[:], scalar=-2.0, in1=cos_half[:],
+        op0=ALU.mult, op1=ALU.mult,
+    )
+    cos_less_1 = pool.tile(shape, F32, name="cos_less_1")
+    nc.vector.scalar_tensor_tensor(
+        out=cos_less_1[:], in0=sin_half[:], scalar=-2.0, in1=sin_half[:],
+        op0=ALU.mult, op1=ALU.mult,
+    )
+    nc.vector.tensor_scalar_add(out=entry[:, :, 0, :, 0], in0=cos_less_1[:], scalar1=1.0)
+    nc.vector.tensor_scalar_add(out=entry[:, :, 1, :, 1], in0=cos_less_1[:], scalar1=1.0)
+    return table
+
+
+def tile_progenattention_pa_kernel(tc, hidden_states, W_qkv, out_0, out_1, out_2):
+    nc = tc.nc
+
+    x_dram = hidden_states.rearrange("b s k -> (b s) k").rearrange(
+        "(p t) k -> p t k", t=TOKEN_TILES
+    )
+    out_dram = [
+        out.rearrange("b s h d -> (b s) (h d)").rearrange("(p t) c -> p t c", t=TOKEN_TILES)
+        for out in (out_0, out_1, out_2)
+    ]
+    w_dram = W_qkv.rearrange("(g s p i) k -> s p g (i k)", g=GROUPS, s=3, p=P, i=2)
+
+    with ExitStack() as ctx:
+        consts = ctx.enter_context(tc.tile_pool(name="consts", bufs=1))
+        raw = ctx.enter_context(tc.tile_pool(name="raw", bufs=1))
+        keep = ctx.enter_context(tc.tile_pool(name="keep", bufs=1))
+        stage = ctx.enter_context(tc.tile_pool(name="stage", bufs=3))
+        results = ctx.enter_context(tc.tile_pool(name="results", bufs=8))
+        psum_words = ctx.enter_context(tc.psum_pool(name="psum_words", bufs=4))
+        psum_sums = ctx.enter_context(tc.psum_pool(name="psum_sums", bufs=4))
+
+        x_raw = []
+        for n in range(TOKEN_TILES // 2):
+            x_pair = raw.tile([P, 2, E], BF16, name="x_raw_%d" % n)
+            nc.sync.dma_start(out=x_pair[:], in_=x_dram[:, 2 * n : 2 * n + 2, :])
+            x_raw.append(x_pair)
+        w_raw = {}
+        for s in ORDER:
+            for a in range(HALVES):
+                w_half = raw.tile([P, 2, 2 * E], BF16, name="w_raw_%d_%d" % (s, a))
+                nc.sync.dma_start(out=w_half[:], in_=w_dram[s, :, 2 * a : 2 * a + 2, :])
+                w_raw[(s, a)] = w_half
+
+        identity = consts.tile([P, P], F32, name="identity")
+        make_identity(nc, identity[:])
+        table = build_rope_tables(nc, consts)
+
+        def leave_psum(n, out, in_):
+            if n % 2 == 0:
+                nc.vector.tensor_copy(out=out, in_=in_)
+            else:
+                nc.scalar.copy(out=out, in_=in_)
+
+        x_codes = keep.tile([P, TOKEN_TILES, PASSES * P], U32, name="x_codes", align_bytes=64)
+        x_scales = keep.tile([P, TOKEN_TILES, PASSES * P], U8, name="x_scales", align_bytes=64)
+        for t in range(TOKEN_TILES):
+            words = x_raw[t // 2][:, t % 2, :].bitcast(F32)
+            x_bank = psum_words.tile([P, 4, P], F32, name="x_bank", tag="bank")
+            for b in range(4):
+                nc.tensor.transpose(
+                    out=x_bank[:, b, :], in_=words[:, b * P : (b + 1) * P], identity=identity[:]
+                )
+            x_grouped = stage.tile([P, PASSES * P * 4], BF16, name="x_grouped", align_bytes=64)
+            leave_psum(
+                t,
+                x_grouped[:].bitcast(F32).rearrange("q (c p u) -> q c p u", c=PASSES, u=2),
+                x_bank[:].rearrange("q (c u) p -> q c p u", u=2),
+            )
+            nc.vector.quantize_mx(
+                out=x_codes[:, t, :].bitcast(FP8X4), scales=x_scales[:, t, :], in_=x_grouped[:]
+            )
+
+        w_codes = {}
+        w_scales = {}
+        for s in ORDER:
+            w_codes[s] = keep.tile(
+                [P, HALVES, PASSES, HALF], U32, name="w_codes_%d" % s, align_bytes=64
+            )
+            w_scales[s] = keep.tile(
+                [P, HALVES, PASSES, HALF], U8, name="w_scales_%d" % s, align_bytes=64
+            )
+
+        def prepare_half(s, a):
+            w_grouped = stage.tile([P, PASSES, HALF * 4], BF16, name="w_grouped", align_bytes=64)
+            for c in range(PASSES):
+                for g in range(2):
+                    words = w_raw[(s, a)][:, g, :].bitcast(F32)
+                    w_bank = psum_words.tile([P, 4, P], F32, name="w_bank", tag="bank")
+                    for i in range(2):
+                        for u in range(2):
+                            first = (4 * i + 2 * c + u) * P
+                            nc.tensor.transpose(
+                                out=w_bank[:, 2 * i + u, :],
+                                in_=words[:, first : first + P],
+                                identity=identity[:],
+                            )
+                    columns = w_grouped[:, c, g * 4 * GROUP_ROWS : (g + 1) * 4 * GROUP_ROWS]
+                    leave_psum(
+                        g,
+                        columns.bitcast(F32).rearrange("q (p b) -> q p b", b=4),
+                        w_bank[:].rearrange("q b p -> q p b"),
+                    )
+            for c in range(PASSES):
+                nc.vector.quantize_mx(
+                    out=w_codes[s][:, a, c, :].bitcast(FP8X4),
+                    scales=w_scales[s][:, a, c, :],
+                    in_=w_grouped[:, c, :],
+                )
+
+        def rotate(result, t):
+            x = result[:].rearrange("p (h d) -> p h d", d=DH)[:, :, 0:ROT]
+            shape = [P, 2, HEADS, ROT]
+            products = stage.tile(shape, F32, name="products")
+            nc.vector.tensor_tensor(
+                out=products[:],
+                in0=x.unsqueeze(1).to_broadcast(shape),
+                in1=table[:, t, :, :].unsqueeze(2).to_broadcast(shape),
+                op=ALU.mult,
+            )
+            terms = products[:].rearrange("p r h (j c) -> p h j r c", c=2)
+            nc.vector.tensor_tensor(
+                out=x.rearrange("p h (j r) -> p h j r", r=2),
+                in0=terms[:, :, :, :, 0],
+                in1=terms[:, :, :, :, 1],
+                op=ALU.add,
+            )
+
+        def project(s, t):
+            result = results.tile([P, WIDTH], F32, name="result")
+            for a in range(HALVES):
+                sums = psum_sums.tile([P, HALF], F32, name="sums")
+                for c in range(PASSES):
+                    nc.tensor.matmul_mx(
+                        out=sums[:],
+                        lhsT=x_codes[:, t, c * P : (c + 1) * P].bitcast(FP8X4),
+                        lhsT_scale=x_scales[:, t, c * P : (c + 1) * P],
+                        rhs=w_codes[s][:, a, c, :].bitcast(FP8X4),
+                        rhs_scale=w_scales[s][:, a, c, :],
+                        start=(c == 0),
+                        stop=(c == PASSES - 1),
+                    )
+                nc.scalar.copy(out=result[:, a * HALF : (a + 1) * HALF], in_=sums[:])
+            if s != V:
+                rotate(result, t)
+            nc.sync.dma_start(out=out_dram[s][:, t, :], in_=result[:])
+
+        first = ORDER[0]
+        for a in range(HALVES):
+            prepare_half(first, a)
+        later = [(s, a) for s in ORDER[1:] for a in range(HALVES)]
+        tiles_between = TOKEN_TILES // len(later)
+        for s in ORDER:
+            for t in range(TOKEN_TILES):
+                project(s, t)
+                if s == first and t % tiles_between == tiles_between - 1:
+                    prepare_half(*later[t // tiles_between])

@@ -17,8 +17,8 @@ P = 128
 SEQ = 512
 TOKENS = 2 * SEQ
 TOKEN_TILES = TOKENS // P
+TILE_PAIRS = TOKEN_TILES // 2
 E = 1024
-WORDS = E // 2
 PASSES = E // 512
 HEADS = 8
 DH = 128
@@ -30,7 +30,7 @@ GROUP_ROWS = WIDTH // GROUPS
 HALVES = 2
 HALF = WIDTH // HALVES
 Q, K, V = 0, 1, 2
-ORDER = (V, Q, K)
+PSUM_BANKS = 8
 
 FLOPS = 2 * TOKENS * E * 3 * WIDTH
 
@@ -116,21 +116,29 @@ def tile_progenattention_pa_kernel(tc, hidden_states, W_qkv, out_0, out_1, out_2
         raw = ctx.enter_context(tc.tile_pool(name="raw", bufs=1))
         keep = ctx.enter_context(tc.tile_pool(name="keep", bufs=1))
         stage = ctx.enter_context(tc.tile_pool(name="stage", bufs=3))
-        results = ctx.enter_context(tc.tile_pool(name="results", bufs=8))
-        psum_words = ctx.enter_context(tc.psum_pool(name="psum_words", bufs=4))
-        psum_sums = ctx.enter_context(tc.psum_pool(name="psum_sums", bufs=4))
+        results = ctx.enter_context(tc.tile_pool(name="results", bufs=TOKEN_TILES + 4))
+        psum = ctx.enter_context(tc.psum_pool(name="psum", bufs=PSUM_BANKS))
+        ctx.enter_context(tc.manual_schedule())
 
-        x_raw = []
-        for n in range(TOKEN_TILES // 2):
-            x_pair = raw.tile([P, 2, E], BF16, name="x_raw_%d" % n)
-            nc.sync.dma_start(out=x_pair[:], in_=x_dram[:, 2 * n : 2 * n + 2, :])
-            x_raw.append(x_pair)
+        x_pairs = list(range(TILE_PAIRS))
+        w_halves = [(s, a) for s in (V, Q, K) for a in range(HALVES)]
+        x_raw = {}
         w_raw = {}
-        for s in ORDER:
-            for a in range(HALVES):
-                w_half = raw.tile([P, 2, 2 * E], BF16, name="w_raw_%d_%d" % (s, a))
-                nc.sync.dma_start(out=w_half[:], in_=w_dram[s, :, 2 * a : 2 * a + 2, :])
-                w_raw[(s, a)] = w_half
+
+        def load_x(n):
+            x_raw[n] = raw.tile([P, 2, E], BF16, name="x_raw_%d" % n)
+            nc.sync.dma_start(out=x_raw[n][:], in_=x_dram[:, 2 * n : 2 * n + 2, :])
+
+        def load_w(s, a):
+            w_raw[(s, a)] = raw.tile([P, 2, 2 * E], BF16, name="w_raw_%d_%d" % (s, a))
+            nc.sync.dma_start(out=w_raw[(s, a)][:], in_=w_dram[s, :, 2 * a : 2 * a + 2, :])
+
+        load_x(x_pairs[0])
+        load_w(*w_halves[0])
+        for n in x_pairs[1:]:
+            load_x(n)
+        for s, a in w_halves[1:]:
+            load_w(s, a)
 
         identity = consts.tile([P, P], F32, name="identity")
         make_identity(nc, identity[:])
@@ -142,28 +150,33 @@ def tile_progenattention_pa_kernel(tc, hidden_states, W_qkv, out_0, out_1, out_2
             else:
                 nc.scalar.copy(out=out, in_=in_)
 
-        x_codes = keep.tile([P, TOKEN_TILES, PASSES * P], U32, name="x_codes", align_bytes=64)
-        x_scales = keep.tile([P, TOKEN_TILES, PASSES * P], U8, name="x_scales", align_bytes=64)
-        for t in range(TOKEN_TILES):
-            words = x_raw[t // 2][:, t % 2, :].bitcast(F32)
-            x_bank = psum_words.tile([P, 4, P], F32, name="x_bank", tag="bank")
-            for b in range(4):
-                nc.tensor.transpose(
-                    out=x_bank[:, b, :], in_=words[:, b * P : (b + 1) * P], identity=identity[:]
+        x_codes = keep.tile([P, TOKEN_TILES * PASSES * P], U32, name="x_codes", align_bytes=64)
+        x_scales = keep.tile([P, TOKEN_TILES * PASSES * P], U8, name="x_scales", align_bytes=64)
+
+        def prepare_x(n):
+            x_grouped = stage.tile([P, 2, PASSES * P * 4], BF16, name="x_grouped", align_bytes=64)
+            for i in range(2):
+                words = x_raw[n][:, i, :].bitcast(F32)
+                x_bank = psum.tile([P, 4, P], F32, name="x_bank", tag="bank")
+                for b in range(4):
+                    nc.tensor.transpose(
+                        out=x_bank[:, b, :], in_=words[:, b * P : (b + 1) * P], identity=identity[:]
+                    )
+                leave_psum(
+                    i,
+                    x_grouped[:, i, :].bitcast(F32).rearrange("q (c p u) -> q c p u", c=PASSES, u=2),
+                    x_bank[:].rearrange("q (c u) p -> q c p u", u=2),
                 )
-            x_grouped = stage.tile([P, PASSES * P * 4], BF16, name="x_grouped", align_bytes=64)
-            leave_psum(
-                t,
-                x_grouped[:].bitcast(F32).rearrange("q (c p u) -> q c p u", c=PASSES, u=2),
-                x_bank[:].rearrange("q (c u) p -> q c p u", u=2),
-            )
+            both_tiles = slice(2 * n * PASSES * P, 2 * (n + 1) * PASSES * P)
             nc.vector.quantize_mx(
-                out=x_codes[:, t, :].bitcast(FP8X4), scales=x_scales[:, t, :], in_=x_grouped[:]
+                out=x_codes[:, both_tiles].bitcast(FP8X4),
+                scales=x_scales[:, both_tiles],
+                in_=x_grouped[:].rearrange("q i k -> q (i k)"),
             )
 
         w_codes = {}
         w_scales = {}
-        for s in ORDER:
+        for s in (V, Q, K):
             w_codes[s] = keep.tile(
                 [P, HALVES, PASSES, HALF], U32, name="w_codes_%d" % s, align_bytes=64
             )
@@ -171,12 +184,12 @@ def tile_progenattention_pa_kernel(tc, hidden_states, W_qkv, out_0, out_1, out_2
                 [P, HALVES, PASSES, HALF], U8, name="w_scales_%d" % s, align_bytes=64
             )
 
-        def prepare_half(s, a):
+        def prepare_w(s, a):
             w_grouped = stage.tile([P, PASSES, HALF * 4], BF16, name="w_grouped", align_bytes=64)
             for c in range(PASSES):
                 for g in range(2):
                     words = w_raw[(s, a)][:, g, :].bitcast(F32)
-                    w_bank = psum_words.tile([P, 4, P], F32, name="w_bank", tag="bank")
+                    w_bank = psum.tile([P, 4, P], F32, name="w_bank", tag="bank")
                     for i in range(2):
                         for u in range(2):
                             first = (4 * i + 2 * c + u) * P
@@ -185,10 +198,10 @@ def tile_progenattention_pa_kernel(tc, hidden_states, W_qkv, out_0, out_1, out_2
                                 in_=words[:, first : first + P],
                                 identity=identity[:],
                             )
-                    columns = w_grouped[:, c, g * 4 * GROUP_ROWS : (g + 1) * 4 * GROUP_ROWS]
+                    group = w_grouped[:, c, g * 4 * GROUP_ROWS : (g + 1) * 4 * GROUP_ROWS]
                     leave_psum(
                         g,
-                        columns.bitcast(F32).rearrange("q (p b) -> q p b", b=4),
+                        group.bitcast(F32).rearrange("q (p b) -> q p b", b=4),
                         w_bank[:].rearrange("q b p -> q p b"),
                     )
             for c in range(PASSES):
@@ -198,50 +211,73 @@ def tile_progenattention_pa_kernel(tc, hidden_states, W_qkv, out_0, out_1, out_2
                     in_=w_grouped[:, c, :],
                 )
 
-        def rotate(result, t):
-            x = result[:].rearrange("p (h d) -> p h d", d=DH)[:, :, 0:ROT]
+        def project_half(s, a, t, result):
+            sums = psum.tile([P, HALF], F32, name="sums", tag="bank")
+            for c in range(PASSES):
+                tokens = slice((PASSES * t + c) * P, (PASSES * t + c + 1) * P)
+                nc.tensor.matmul_mx(
+                    out=sums[:],
+                    lhsT=x_codes[:, tokens].bitcast(FP8X4),
+                    lhsT_scale=x_scales[:, tokens],
+                    rhs=w_codes[s][:, a, c, :].bitcast(FP8X4),
+                    rhs_scale=w_scales[s][:, a, c, :],
+                    start=(c == 0),
+                    stop=(c == PASSES - 1),
+                )
+            nc.scalar.copy(out=result[:, a * HALF : (a + 1) * HALF], in_=sums[:])
+
+        def store(s, t, result):
+            nc.sync.dma_start(out=out_dram[s][:, t, :], in_=result[:])
+
+        def rotated_part(result):
+            return result[:].rearrange("p (h d) -> p h d", d=DH)[:, :, 0:ROT]
+
+        def rotation_products(result, t):
             shape = [P, 2, HEADS, ROT]
             products = stage.tile(shape, F32, name="products")
             nc.vector.tensor_tensor(
                 out=products[:],
-                in0=x.unsqueeze(1).to_broadcast(shape),
+                in0=rotated_part(result).unsqueeze(1).to_broadcast(shape),
                 in1=table[:, t, :, :].unsqueeze(2).to_broadcast(shape),
                 op=ALU.mult,
             )
+            return products
+
+        def rotation_sums(result, products):
             terms = products[:].rearrange("p r h (j c) -> p h j r c", c=2)
             nc.vector.tensor_tensor(
-                out=x.rearrange("p h (j r) -> p h j r", r=2),
+                out=rotated_part(result).rearrange("p h (j r) -> p h j r", r=2),
                 in0=terms[:, :, :, :, 0],
                 in1=terms[:, :, :, :, 1],
                 op=ALU.add,
             )
 
-        def project(s, t):
-            result = results.tile([P, WIDTH], F32, name="result")
-            for a in range(HALVES):
-                sums = psum_sums.tile([P, HALF], F32, name="sums")
-                for c in range(PASSES):
-                    nc.tensor.matmul_mx(
-                        out=sums[:],
-                        lhsT=x_codes[:, t, c * P : (c + 1) * P].bitcast(FP8X4),
-                        lhsT_scale=x_scales[:, t, c * P : (c + 1) * P],
-                        rhs=w_codes[s][:, a, c, :].bitcast(FP8X4),
-                        rhs_scale=w_scales[s][:, a, c, :],
-                        start=(c == 0),
-                        stop=(c == PASSES - 1),
-                    )
-                nc.scalar.copy(out=result[:, a * HALF : (a + 1) * HALF], in_=sums[:])
-            if s != V:
-                rotate(result, t)
-            nc.sync.dma_start(out=out_dram[s][:, t, :], in_=result[:])
-
-        first = ORDER[0]
+        prepare_x(x_pairs[0])
+        prepare_w(*w_halves[0])
+        later = [(prepare_x, (n,)) for n in x_pairs[1:]] + [(prepare_w, h) for h in w_halves[1:]]
+        assert len(later) == HALVES * TILE_PAIRS
+        v_result = [results.tile([P, WIDTH], F32, name="result") for t in range(TOKEN_TILES)]
         for a in range(HALVES):
-            prepare_half(first, a)
-        later = [(s, a) for s in ORDER[1:] for a in range(HALVES)]
-        tiles_between = TOKEN_TILES // len(later)
-        for s in ORDER:
+            for n in x_pairs:
+                prepare, piece = later[a * TILE_PAIRS + n]
+                prepare(*piece)
+                for t in (2 * n, 2 * n + 1):
+                    project_half(V, a, t, v_result[t])
+                    if a == HALVES - 1:
+                        store(V, t, v_result[t])
+
+        def finish(s, t, result, products):
+            rotation_sums(result, products)
+            store(s, t, result)
+
+        behind = None
+        for s in (Q, K):
             for t in range(TOKEN_TILES):
-                project(s, t)
-                if s == first and t % tiles_between == tiles_between - 1:
-                    prepare_half(*later[t // tiles_between])
+                result = results.tile([P, WIDTH], F32, name="result")
+                for a in range(HALVES):
+                    project_half(s, a, t, result)
+                products = rotation_products(result, t)
+                if behind is not None:
+                    finish(*behind)
+                behind = (s, t, result, products)
+        finish(*behind)

@@ -109,13 +109,13 @@ def tile_progenattention_pa_kernel(tc, hidden_states, W_qkv, out_0, out_1, out_2
         out.rearrange("b s h d -> (b s) (h d)").rearrange("(p t) c -> p t c", t=TOKEN_TILES)
         for out in (out_0, out_1, out_2)
     ]
-    w_dram = W_qkv.rearrange("(g s p i) k -> s p g (i k)", g=GROUPS, s=3, p=P, i=2)
+    w_dram = W_qkv.rearrange("(g s p i) k -> s g p (i k)", g=GROUPS, s=3, p=P, i=2)
 
     with ExitStack() as ctx:
         consts = ctx.enter_context(tc.tile_pool(name="consts", bufs=1))
         raw = ctx.enter_context(tc.tile_pool(name="raw", bufs=1))
         keep = ctx.enter_context(tc.tile_pool(name="keep", bufs=1))
-        stage = ctx.enter_context(tc.tile_pool(name="stage", bufs=3))
+        stage = ctx.enter_context(tc.tile_pool(name="stage", bufs=4))
         results = ctx.enter_context(tc.tile_pool(name="results", bufs=TOKEN_TILES + 4))
         psum = ctx.enter_context(tc.psum_pool(name="psum", bufs=PSUM_BANKS))
         ctx.enter_context(tc.manual_schedule())
@@ -130,8 +130,9 @@ def tile_progenattention_pa_kernel(tc, hidden_states, W_qkv, out_0, out_1, out_2
             nc.sync.dma_start(out=x_raw[n][:], in_=x_dram[:, 2 * n : 2 * n + 2, :])
 
         def load_w(s, a):
-            w_raw[(s, a)] = raw.tile([P, 2, 2 * E], BF16, name="w_raw_%d_%d" % (s, a))
-            nc.sync.dma_start(out=w_raw[(s, a)][:], in_=w_dram[s, :, 2 * a : 2 * a + 2, :])
+            for g in (2 * a, 2 * a + 1):
+                w_raw[(s, g)] = raw.tile([P, 2 * E], BF16, name="w_raw_%d_%d" % (s, g))
+                nc.sync.dma_start(out=w_raw[(s, g)][:], in_=w_dram[s, g, :, :])
 
         load_x(x_pairs[0])
         load_w(*w_halves[0])
@@ -186,9 +187,9 @@ def tile_progenattention_pa_kernel(tc, hidden_states, W_qkv, out_0, out_1, out_2
 
         def prepare_w(s, a):
             w_grouped = stage.tile([P, PASSES, HALF * 4], BF16, name="w_grouped", align_bytes=64)
-            for c in range(PASSES):
-                for g in range(2):
-                    words = w_raw[(s, a)][:, g, :].bitcast(F32)
+            for g in range(2):
+                words = w_raw[(s, 2 * a + g)][:].bitcast(F32)
+                for c in range(PASSES):
                     w_bank = psum.tile([P, 4, P], F32, name="w_bank", tag="bank")
                     for i in range(2):
                         for u in range(2):
@@ -200,7 +201,7 @@ def tile_progenattention_pa_kernel(tc, hidden_states, W_qkv, out_0, out_1, out_2
                             )
                     group = w_grouped[:, c, g * 4 * GROUP_ROWS : (g + 1) * 4 * GROUP_ROWS]
                     leave_psum(
-                        g,
+                        g + c,
                         group.bitcast(F32).rearrange("q (p b) -> q p b", b=4),
                         w_bank[:].rearrange("q b p -> q p b"),
                     )
@@ -229,24 +230,25 @@ def tile_progenattention_pa_kernel(tc, hidden_states, W_qkv, out_0, out_1, out_2
         def store(s, t, result):
             nc.sync.dma_start(out=out_dram[s][:, t, :], in_=result[:])
 
-        def rotated_part(result):
-            return result[:].rearrange("p (h d) -> p h d", d=DH)[:, :, 0:ROT]
+        def rotated_part(result, a):
+            half = result[:, a * HALF : (a + 1) * HALF]
+            return half.rearrange("p (h d) -> p h d", d=DH)[:, :, 0:ROT]
 
-        def rotation_products(result, t):
-            shape = [P, 2, HEADS, ROT]
+        def rotation_products(result, t, a):
+            shape = [P, 2, HEADS // HALVES, ROT]
             products = stage.tile(shape, F32, name="products")
             nc.vector.tensor_tensor(
                 out=products[:],
-                in0=rotated_part(result).unsqueeze(1).to_broadcast(shape),
+                in0=rotated_part(result, a).unsqueeze(1).to_broadcast(shape),
                 in1=table[:, t, :, :].unsqueeze(2).to_broadcast(shape),
                 op=ALU.mult,
             )
             return products
 
-        def rotation_sums(result, products):
+        def rotation_sums(result, a, products):
             terms = products[:].rearrange("p r h (j c) -> p h j r c", c=2)
             nc.vector.tensor_tensor(
-                out=rotated_part(result).rearrange("p h (j r) -> p h j r", r=2),
+                out=rotated_part(result, a).rearrange("p h (j r) -> p h j r", r=2),
                 in0=terms[:, :, :, :, 0],
                 in1=terms[:, :, :, :, 1],
                 op=ALU.add,
@@ -266,18 +268,12 @@ def tile_progenattention_pa_kernel(tc, hidden_states, W_qkv, out_0, out_1, out_2
                     if a == HALVES - 1:
                         store(V, t, v_result[t])
 
-        def finish(s, t, result, products):
-            rotation_sums(result, products)
-            store(s, t, result)
-
-        behind = None
         for s in (Q, K):
             for t in range(TOKEN_TILES):
                 result = results.tile([P, WIDTH], F32, name="result")
                 for a in range(HALVES):
                     project_half(s, a, t, result)
-                products = rotation_products(result, t)
-                if behind is not None:
-                    finish(*behind)
-                behind = (s, t, result, products)
-        finish(*behind)
+                products = [rotation_products(result, t, a) for a in range(HALVES)]
+                for a in range(HALVES):
+                    rotation_sums(result, a, products[a])
+                store(s, t, result)

import math
from contextlib import ExitStack

import concourse.mybir as mybir
from concourse.masks import make_identity

F32 = mybir.dt.float32
BF16 = mybir.dt.bfloat16
I32 = mybir.dt.int32
U32 = mybir.dt.uint32
U8 = mybir.dt.uint8
FP8X4 = mybir.dt.float8_e4m3fn_x4
ALU = mybir.AluOpType
ACT = mybir.ActivationFunctionType

P = 128
SEQ = 512
TOKENS = 2 * SEQ
TOKEN_TILES = TOKENS // P
TILE_PAIRS = TOKEN_TILES // 2
E = 1024
PASSES = E // 512
HEADS = 8
DH = 128
ROT = 32
PAIRS = ROT // 2
WIDTH = HEADS * DH
GROUPS = 4
GROUP_ROWS = WIDTH // GROUPS
HALVES = 2
HALF = WIDTH // HALVES
Q, K, V = 0, 1, 2
PSUM_BANKS = 8

FLOPS = 2 * TOKENS * E * 3 * WIDTH

ROUND_MAGIC = 1.5 * 2.0**23
TURN_HI = 6.28125
TURN_LO = 2.0 * math.pi - TURN_HI


def build_rope_tables(nc, pool):
    token = pool.tile([P, TOKEN_TILES], I32, name="token")
    nc.gpsimd.iota(token[:], pattern=[[1, TOKEN_TILES]], base=0, channel_multiplier=TOKEN_TILES)
    position_i = pool.tile([P, TOKEN_TILES], I32, name="position_i")
    nc.vector.tensor_single_scalar(out=position_i[:], in_=token[:], scalar=SEQ - 1, op=ALU.bitwise_and)
    position = pool.tile([P, TOKEN_TILES], F32, name="position")
    nc.vector.tensor_copy(out=position[:], in_=position_i[:])

    shape = [P, TOKEN_TILES, PAIRS]
    angle = pool.tile(shape, F32, name="angle")
    for j in range(PAIRS):
        nc.vector.tensor_scalar_mul(
            out=angle[:, :, j], in0=position[:], scalar1=10000.0 ** (-2.0 * j / ROT)
        )
    turns = pool.tile(shape, F32, name="turns")
    nc.vector.tensor_scalar(
        out=turns[:], in0=angle[:], scalar1=0.5 / math.pi, scalar2=ROUND_MAGIC,
        op0=ALU.mult, op1=ALU.add,
    )
    nc.vector.tensor_scalar_sub(out=turns[:], in0=turns[:], scalar1=ROUND_MAGIC)
    partly = pool.tile(shape, F32, name="partly")
    nc.vector.scalar_tensor_tensor(
        out=partly[:], in0=turns[:], scalar=-TURN_HI, in1=angle[:], op0=ALU.mult, op1=ALU.add
    )
    reduced = pool.tile(shape, F32, name="reduced")
    nc.vector.scalar_tensor_tensor(
        out=reduced[:], in0=turns[:], scalar=-TURN_LO, in1=partly[:], op0=ALU.mult, op1=ALU.add
    )
    sin_half = pool.tile(shape, F32, name="sin_half")
    nc.scalar.activation(out=sin_half[:], in_=reduced[:], func=ACT.Sin, scale=0.5)
    size = pool.tile(shape, F32, name="size")
    nc.vector.scalar_tensor_tensor(
        out=size[:], in0=reduced[:], scalar=-1.0, in1=reduced[:], op0=ALU.mult, op1=ALU.max
    )
    nc.vector.tensor_scalar(
        out=size[:], in0=size[:], scalar1=-0.5, scalar2=0.5 * math.pi, op0=ALU.mult, op1=ALU.add
    )
    cos_half = pool.tile(shape, F32, name="cos_half")
    nc.scalar.activation(out=cos_half[:], in_=size[:], func=ACT.Sin)

    table = pool.tile([P, TOKEN_TILES, 2, ROT], F32, name="table")
    entry = table[:].rearrange("p t r (j c) -> p t r j c", c=2)
    nc.vector.scalar_tensor_tensor(
        out=entry[:, :, 1, :, 0], in0=sin_half[:], scalar=2.0, in1=cos_half[:],
        op0=ALU.mult, op1=ALU.mult,
    )
    nc.vector.scalar_tensor_tensor(
        out=entry[:, :, 0, :, 1], in0=sin_half[:], scalar=-2.0, in1=cos_half[:],
        op0=ALU.mult, op1=ALU.mult,
    )
    cos_less_1 = pool.tile(shape, F32, name="cos_less_1")
    nc.vector.scalar_tensor_tensor(
        out=cos_less_1[:], in0=sin_half[:], scalar=-2.0, in1=sin_half[:],
        op0=ALU.mult, op1=ALU.mult,
    )
    nc.vector.tensor_scalar_add(out=entry[:, :, 0, :, 0], in0=cos_less_1[:], scalar1=1.0)
    nc.vector.tensor_scalar_add(out=entry[:, :, 1, :, 1], in0=cos_less_1[:], scalar1=1.0)
    return table


def tile_progenattention_pa_kernel(tc, hidden_states, W_qkv, out_0, out_1, out_2):
    nc = tc.nc

    x_dram = hidden_states.rearrange("b s k -> (b s) k").rearrange(
        "(p t) k -> p t k", t=TOKEN_TILES
    )
    out_dram = [
        out.rearrange("b s h d -> (b s) (h d)").rearrange("(p t) c -> p t c", t=TOKEN_TILES)
        for out in (out_0, out_1, out_2)
    ]
    w_dram = W_qkv.rearrange("(g s p i) k -> s g p (i k)", g=GROUPS, s=3, p=P, i=2)

    with ExitStack() as ctx:
        consts = ctx.enter_context(tc.tile_pool(name="consts", bufs=1))
        raw = ctx.enter_context(tc.tile_pool(name="raw", bufs=1))
        keep = ctx.enter_context(tc.tile_pool(name="keep", bufs=1))
        stage = ctx.enter_context(tc.tile_pool(name="stage", bufs=4))
        results = ctx.enter_context(tc.tile_pool(name="results", bufs=TOKEN_TILES + 4))
        psum = ctx.enter_context(tc.psum_pool(name="psum", bufs=PSUM_BANKS))
        ctx.enter_context(tc.manual_schedule())

        x_pairs = list(range(TILE_PAIRS))
        w_halves = [(s, a) for s in (V, Q, K) for a in range(HALVES)]
        x_raw = {}
        w_raw = {}

        def load_x(n):
            x_raw[n] = raw.tile([P, 2, E], BF16, name="x_raw_%d" % n)
            nc.sync.dma_start(out=x_raw[n][:], in_=x_dram[:, 2 * n : 2 * n + 2, :])

        def load_w(s, a):
            for g in (2 * a, 2 * a + 1):
                w_raw[(s, g)] = raw.tile([P, 2 * E], BF16, name="w_raw_%d_%d" % (s, g))
                nc.sync.dma_start(out=w_raw[(s, g)][:], in_=w_dram[s, g, :, :])

        load_x(x_pairs[0])
        load_w(*w_halves[0])
        for n in x_pairs[1:]:
            load_x(n)
        for s, a in w_halves[1:]:
            load_w(s, a)

        identity = consts.tile([P, P], F32, name="identity")
        make_identity(nc, identity[:])
        table = build_rope_tables(nc, consts)

        def leave_psum(n, out, in_):
            if n % 2 == 0:
                nc.vector.tensor_copy(out=out, in_=in_)
            else:
                nc.scalar.copy(out=out, in_=in_)

        x_codes = keep.tile([P, TOKEN_TILES * PASSES * P], U32, name="x_codes", align_bytes=64)
        x_scales = keep.tile([P, TOKEN_TILES * PASSES * P], U8, name="x_scales", align_bytes=64)

        def prepare_x(n):
            x_grouped = stage.tile([P, 2, PASSES * P * 4], BF16, name="x_grouped", align_bytes=64)
            for i in range(2):
                words = x_raw[n][:, i, :].bitcast(F32)
                x_bank = psum.tile([P, 4, P], F32, name="x_bank", tag="bank")
                for b in range(4):
                    nc.tensor.transpose(
                        out=x_bank[:, b, :], in_=words[:, b * P : (b + 1) * P], identity=identity[:]
                    )
                leave_psum(
                    i,
                    x_grouped[:, i, :].bitcast(F32).rearrange("q (c p u) -> q c p u", c=PASSES, u=2),
                    x_bank[:].rearrange("q (c u) p -> q c p u", u=2),
                )
            both_tiles = slice(2 * n * PASSES * P, 2 * (n + 1) * PASSES * P)
            nc.vector.quantize_mx(
                out=x_codes[:, both_tiles].bitcast(FP8X4),
                scales=x_scales[:, both_tiles],
                in_=x_grouped[:].rearrange("q i k -> q (i k)"),
            )

        w_codes = {}
        w_scales = {}
        for s in (V, Q, K):
            w_codes[s] = keep.tile(
                [P, HALVES, PASSES, HALF], U32, name="w_codes_%d" % s, align_bytes=64
            )
            w_scales[s] = keep.tile(
                [P, HALVES, PASSES, HALF], U8, name="w_scales_%d" % s, align_bytes=64
            )

        def prepare_w(s, a):
            w_grouped = stage.tile([P, PASSES, HALF * 4], BF16, name="w_grouped", align_bytes=64)
            for g in range(2):
                words = w_raw[(s, 2 * a + g)][:].bitcast(F32)
                for c in range(PASSES):
                    w_bank = psum.tile([P, 4, P], F32, name="w_bank", tag="bank")
                    for i in range(2):
                        for u in range(2):
                            first = (4 * i + 2 * c + u) * P
                            nc.tensor.transpose(
                                out=w_bank[:, 2 * i + u, :],
                                in_=words[:, first : first + P],
                                identity=identity[:],
                            )
                    group = w_grouped[:, c, g * 4 * GROUP_ROWS : (g + 1) * 4 * GROUP_ROWS]
                    leave_psum(
                        g + c,
                        group.bitcast(F32).rearrange("q (p b) -> q p b", b=4),
                        w_bank[:].rearrange("q b p -> q p b"),
                    )
            for c in range(PASSES):
                nc.vector.quantize_mx(
                    out=w_codes[s][:, a, c, :].bitcast(FP8X4),
                    scales=w_scales[s][:, a, c, :],
                    in_=w_grouped[:, c, :],
                )

        def project_half(s, a, t, result):
            sums = psum.tile([P, HALF], F32, name="sums", tag="bank")
            for c in range(PASSES):
                tokens = slice((PASSES * t + c) * P, (PASSES * t + c + 1) * P)
                nc.tensor.matmul_mx(
                    out=sums[:],
                    lhsT=x_codes[:, tokens].bitcast(FP8X4),
                    lhsT_scale=x_scales[:, tokens],
                    rhs=w_codes[s][:, a, c, :].bitcast(FP8X4),
                    rhs_scale=w_scales[s][:, a, c, :],
                    start=(c == 0),
                    stop=(c == PASSES - 1),
                )
            nc.scalar.copy(out=result[:, a * HALF : (a + 1) * HALF], in_=sums[:])

        def store(s, t, result):
            nc.sync.dma_start(out=out_dram[s][:, t, :], in_=result[:])

        def rotated_part(result, a):
            half = result[:, a * HALF : (a + 1) * HALF]
            return half.rearrange("p (h d) -> p h d", d=DH)[:, :, 0:ROT]

        def rotation_products(result, t, a):
            shape = [P, 2, HEADS // HALVES, ROT]
            products = stage.tile(shape, F32, name="products")
            nc.vector.tensor_tensor(
                out=products[:],
                in0=rotated_part(result, a).unsqueeze(1).to_broadcast(shape),
                in1=table[:, t, :, :].unsqueeze(2).to_broadcast(shape),
                op=ALU.mult,
            )
            return products

        def rotation_sums(result, a, products):
            terms = products[:].rearrange("p r h (j c) -> p h j r c", c=2)
            nc.vector.tensor_tensor(
                out=rotated_part(result, a).rearrange("p h (j r) -> p h j r", r=2),
                in0=terms[:, :, :, :, 0],
                in1=terms[:, :, :, :, 1],
                op=ALU.add,
            )

        prepare_x(x_pairs[0])
        prepare_w(*w_halves[0])
        later = [(prepare_x, (n,)) for n in x_pairs[1:]] + [(prepare_w, h) for h in w_halves[1:]]
        assert len(later) == HALVES * TILE_PAIRS
        v_result = [results.tile([P, WIDTH], F32, name="result") for t in range(TOKEN_TILES)]
        for a in range(HALVES):
            for n in x_pairs:
                prepare, piece = later[a * TILE_PAIRS + n]
                prepare(*piece)
                for t in (2 * n, 2 * n + 1):
                    project_half(V, a, t, v_result[t])
                    if a == HALVES - 1:
                        store(V, t, v_result[t])

        for s in (Q, K):
            for t in range(TOKEN_TILES):
                result = results.tile([P, WIDTH], F32, name="result")
                for a in range(HALVES):
                    project_half(s, a, t, result)
                products = [rotation_products(result, t, a) for a in range(HALVES)]
                for a in range(HALVES):
                    rotation_sums(result, a, products[a])
                store(s, t, result)
